import numpy as np
import ml_dtypes


def mxq(x, axis, fmt="e4m3"):
    dtype, down = {"e4m3": (ml_dtypes.float8_e4m3fn, 7), "e5m2": (ml_dtypes.float8_e5m2, 14)}[fmt]
    v = np.moveaxis(np.asarray(x, np.float32).astype(ml_dtypes.bfloat16).astype(np.float64), axis, -1)
    blocks = v.reshape(v.shape[:-1] + (-1, 32))
    amax = np.abs(blocks).max(-1, keepdims=True)
    byte = np.maximum(np.where(amax > 0, np.frexp(amax)[1] - 1 + 127, 0) - down, 1)
    scale = np.exp2(byte - 127.0)
    codes = (blocks / scale).astype(np.float32).astype(dtype).astype(np.float64)
    return np.moveaxis((codes * scale).reshape(v.shape), -1, axis)


WIDE = False


def mx_kscale(k):
    if not WIDE:
        return np.ones(k)
    levels = np.array([10, -10, 5, -5, 0])
    a = np.random.permutation(np.resize(levels, k // 512 * 4)).reshape(k // 512, 4)
    idx = np.arange(k)
    return np.exp2(a[idx // 512, idx % 128 // 32])


BF16 = ml_dtypes.bfloat16


def bf(x):
    return np.asarray(x, np.float32).astype(BF16)


def f64(x):
    return np.asarray(x).astype(np.float64)


BATCH, OUTPUT_R, KERNEL, INPUT_DEPTH, OUTPUT_DEPTH, SIX = 1024, 2, 8, 8, 64, 6
INPUT_R = OUTPUT_R * KERNEL
P = OUTPUT_R ** 2
G = OUTPUT_DEPTH * SIX
W = KERNEL ** 2 * INPUT_DEPTH
ROWS = P * G
COLS = INPUT_R ** 2 * INPUT_DEPTH
IDX = np.arange(COLS).reshape(OUTPUT_R, KERNEL, OUTPUT_R, KERNEL * INPUT_DEPTH).transpose(0, 2, 1, 3).reshape(P, W)


def setup_inputs():
    s = mx_kscale(W)
    sc = np.empty(COLS)
    sc[IDX] = s
    c = np.mean(1.0 / s)
    window = np.zeros((P, COLS))
    window[np.arange(P)[:, None], IDX] = 1.0
    return {"x": bf(np.random.standard_normal((BATCH, COLS)) * 0.2 * np.sqrt(W) * c * sc),
            "connect_w": bf(np.random.standard_normal((ROWS, COLS))),
            "connect_mask": bf(np.random.uniform(0.5, 1.5, (ROWS, COLS)) * np.repeat(window, G, axis=0) / sc)}


def reference(x, connect_w, connect_mask):
    w = np.exp(f64(connect_w)) * f64(connect_mask)
    w = w / np.sum(w, axis=-1, keepdims=True)
    xw = f64(x)[:, IDX].transpose(1, 0, 2)
    ww = np.take_along_axis(w.reshape(P, G, COLS), IDX[:, None, :], axis=2)
    out = mxq(xw, 2, "e4m3") @ mxq(ww, 2, "e4m3").transpose(0, 2, 1)
    return out.transpose(1, 0, 2).reshape(BATCH, -1, SIX)

@@ -1,0 +1,167 @@
+from contextlib import ExitStack
+
+import concourse.mybir as mybir
+from concourse.masks import make_identity
+
+F32 = mybir.dt.float32
+BF16 = mybir.dt.bfloat16
+U32 = mybir.dt.uint32
+U8 = mybir.dt.uint8
+FP8X4 = mybir.dt.float8_e4m3fn_x4
+ACT = mybir.ActivationFunctionType
+ALU = mybir.AluOpType
+
+P = 128
+PACK = 4
+K = P * PACK
+BANK = 512
+
+BATCH = 1024
+COLS = 2048
+PIXEL_ROWS = 16
+ROW = COLS // PIXEL_ROWS
+RUN = ROW // 2
+WINDOW_ROWS = PIXEL_ROWS // 2
+WINDOWS = 4
+G = 384
+OUT_COLS = WINDOWS * G
+HALF = COLS // 2
+SPAN = HALF - RUN
+
+W_TILES = OUT_COLS // P
+X_TILES = BATCH // P
+BANKS_OUT = OUT_COLS // BANK
+
+CUTS = sorted(set(range(0, OUT_COLS + 1, G)) | set(range(0, OUT_COLS + 1, BANK // 2)))
+
+FLOPS = 2 * BATCH * OUT_COLS * K
+BYTES = 2 * BATCH * COLS + 2 * 2 * OUT_COLS * K + 4 * BATCH * OUT_COLS
+
+
+def window_view(half_rows):
+    return half_rows[:].rearrange("g (a s) -> g a s", s=ROW)[:, :, 0:RUN]
+
+
+def tile_connectlayer_kernel(tc, x, connect_w, connect_mask, out):
+    nc = tc.nc
+    out_rows = out.rearrange("b r s -> b (r s)")
+
+    with ExitStack() as ctx:
+        const = ctx.enter_context(tc.tile_pool(name="const", bufs=1))
+        loads = ctx.enter_context(tc.tile_pool(name="loads", bufs=1))
+        keep = ctx.enter_context(tc.tile_pool(name="keep", bufs=1))
+        work = ctx.enter_context(tc.tile_pool(name="work", bufs=3))
+        transposed = ctx.enter_context(tc.psum_pool(name="transposed", bufs=4))
+        sums = ctx.enter_context(tc.psum_pool(name="sums", bufs=4))
+
+        cw_in = []
+        mask_in = []
+        for r in range(W_TILES):
+            i, j = divmod(r * P // G, 2)
+            rows = slice(r * P, (r + 1) * P)
+            cols = slice(i * HALF + j * RUN, i * HALF + j * RUN + SPAN)
+            cw_t = loads.tile([P, HALF], BF16, name="cw%d" % r)
+            nc.sync.dma_start(out=cw_t[:, 0:SPAN], in_=connect_w[rows, cols])
+            mask_t = loads.tile([P, HALF], BF16, name="mask%d" % r)
+            nc.sync.dma_start(out=mask_t[:, 0:SPAN], in_=connect_mask[rows, cols])
+            cw_in.append(cw_t)
+            mask_in.append(mask_t)
+        x_in = []
+        for n in range(X_TILES):
+            x_t = loads.tile([P, COLS], BF16, name="x%d" % n)
+            nc.sync.dma_start(out=x_t[:], in_=x[n * P : (n + 1) * P, :])
+            x_in.append(x_t)
+
+        ident_bf = const.tile([P, P], BF16, name="ident_bf")
+        make_identity(nc, ident_bf[:])
+        ident_f32 = const.tile([P, P], F32, name="ident_f32")
+        make_identity(nc, ident_f32[:])
+
+        w_codes = keep.tile([P, OUT_COLS], U32, name="w_codes", align_bytes=64)
+        w_scales = keep.tile([P, OUT_COLS], U8, name="w_scales", align_bytes=64)
+        for r in range(W_TILES):
+            expw = work.tile([P, WINDOW_ROWS, RUN], F32, name="expw")
+            nc.scalar.activation(out=expw[:], in_=window_view(cw_in[r]), func=ACT.Exp)
+            prod = work.tile([P, WINDOW_ROWS, RUN], F32, name="prod")
+            rowsum = work.tile([P, 1], F32, name="rowsum")
+            nc.vector.scalar_tensor_tensor(
+                out=prod[:],
+                in0=expw[:],
+                scalar=1.0,
+                in1=window_view(mask_in[r]),
+                op0=ALU.mult,
+                op1=ALU.mult,
+                accum_out=rowsum[:],
+            )
+            rinv = work.tile([P, 1], F32, name="rinv")
+            nc.vector.reciprocal(out=rinv[:], in_=rowsum[:])
+            w_bf = work.tile([P, PACK, P], BF16, name="w_bf")
+            nc.vector.tensor_scalar(
+                out=w_bf[:].rearrange("g (u e) q -> g u e q", e=2),
+                in0=prod[:].rearrange("g a c -> g (a c)").rearrange("g (u q e) -> g u e q", u=2, e=2),
+                scalar1=rinv[:, 0:1],
+                scalar2=None,
+                op0=ALU.mult,
+            )
+            wt = transposed.tile([P, PACK, P], BF16, name="wt", tag="bank")
+            for t in range(PACK):
+                nc.tensor.transpose(wt[:, t, :], w_bf[:, t, :], ident_bf[:])
+            w_grouped = work.tile([P, P, PACK], BF16, name="w_grouped", align_bytes=64)
+            nc.scalar.copy(out=w_grouped[:], in_=wt[:].rearrange("q t g -> q g t"))
+            nc.vector.quantize_mx(
+                out=w_codes[:, r * P : (r + 1) * P].bitcast(FP8X4),
+                scales=w_scales[:, r * P : (r + 1) * P],
+                in_=w_grouped[:].rearrange("q g t -> q (g t)"),
+            )
+
+        def prepare_x(n):
+            xc = work.tile([P, COLS], BF16, name="xc")
+            nc.vector.tensor_copy(
+                out=xc[:].rearrange("b (j r c) -> b j r c", j=2, c=RUN),
+                in_=x_in[n][:].rearrange("b (r j c) -> b j r c", j=2, c=RUN),
+            )
+            xc_words = xc[:].bitcast(F32)
+            x_grouped = work.tile([P, COLS], BF16, name="x_grouped", align_bytes=64)
+            xg_words = x_grouped[:].bitcast(F32)
+            for j in range(2):
+                xt = transposed.tile([P, PACK, P], F32, name="xt", tag="bank")
+                for iu in range(PACK):
+                    first = (j * PACK + iu) * P
+                    nc.tensor.transpose(xt[:, iu, :], xc_words[:, first : first + P], ident_f32[:])
+                nc.scalar.copy(
+                    out=xg_words[:, j * BANK : (j + 1) * BANK].rearrange("q (i b u) -> q i b u", i=2, u=2),
+                    in_=xt[:].rearrange("q (i u) b -> q i b u", u=2),
+                )
+            x_codes = work.tile([P, BANK], U32, name="x_codes", align_bytes=64)
+            x_scales = work.tile([P, BANK], U8, name="x_scales", align_bytes=64)
+            nc.vector.quantize_mx(out=x_codes[:].bitcast(FP8X4), scales=x_scales[:], in_=x_grouped[:])
+            return x_codes, x_scales
+
+        def multiply_and_store(n, x_codes, x_scales):
+            acc = [sums.tile([P, BANK], F32, name="acc%d" % b, tag="acc") for b in range(BANKS_OUT)]
+            for c0, c1 in zip(CUTS[:-1], CUTS[1:]):
+                i, j = divmod(c0 // G, 2)
+                slot = slice((2 * j + i) * P, (2 * j + i + 1) * P)
+                b = c0 // BANK
+                nc.tensor.matmul_mx(
+                    out=acc[b][:, c0 - b * BANK : c1 - b * BANK],
+                    lhsT=x_codes[:, slot].bitcast(FP8X4),
+                    lhsT_scale=x_scales[:, slot],
+                    rhs=w_codes[:, c0:c1].bitcast(FP8X4),
+                    rhs_scale=w_scales[:, c0:c1],
+                    start=True,
+                    stop=True,
+                )
+            result = work.tile([P, OUT_COLS], F32, name="result")
+            for b in range(BANKS_OUT):
+                if (n * BANKS_OUT + b) % 2 == 0:
+                    nc.scalar.copy(out=result[:, b * BANK : (b + 1) * BANK], in_=acc[b][:])
+                else:
+                    nc.vector.tensor_copy(out=result[:, b * BANK : (b + 1) * BANK], in_=acc[b][:])
+            nc.sync.dma_start(out=out_rows[n * P : (n + 1) * P, :], in_=result[:])
+
+        ready = prepare_x(0)
+        for n in range(X_TILES):
+            following = prepare_x(n + 1) if n + 1 < X_TILES else None
+            multiply_and_store(n, ready[0], ready[1])
+            ready = following

@@ -51,8 +51,10 @@ def tile_connectlayer_kernel(tc, x, connect_w, connect_mask, out):
         loads = ctx.enter_context(tc.tile_pool(name="loads", bufs=1))
         keep = ctx.enter_context(tc.tile_pool(name="keep", bufs=1))
         work = ctx.enter_context(tc.tile_pool(name="work", bufs=3))
-        transposed = ctx.enter_context(tc.psum_pool(name="transposed", bufs=4))
-        sums = ctx.enter_context(tc.psum_pool(name="sums", bufs=4))
+        results = ctx.enter_context(tc.tile_pool(name="results", bufs=4))
+        transposed = ctx.enter_context(tc.psum_pool(name="transposed", bufs=3))
+        sums = ctx.enter_context(tc.psum_pool(name="sums", bufs=5))
+        ctx.enter_context(tc.manual_schedule())
 
         cw_in = []
         mask_in = []
@@ -79,89 +81,136 @@ def tile_connectlayer_kernel(tc, x, connect_w, connect_mask, out):
 
         w_codes = keep.tile([P, OUT_COLS], U32, name="w_codes", align_bytes=64)
         w_scales = keep.tile([P, OUT_COLS], U8, name="w_scales", align_bytes=64)
-        for r in range(W_TILES):
-            expw = work.tile([P, WINDOW_ROWS, RUN], F32, name="expw")
-            nc.scalar.activation(out=expw[:], in_=window_view(cw_in[r]), func=ACT.Exp)
-            prod = work.tile([P, WINDOW_ROWS, RUN], F32, name="prod")
-            rowsum = work.tile([P, 1], F32, name="rowsum")
+
+        expw, prod, rowsum, rinv, w_bf, wt, w_grouped = {}, {}, {}, {}, {}, {}, {}
+        xc, xt, x_grouped, x_codes, x_scales, acc, result = {}, {}, {}, {}, {}, {}, {}
+
+        def exponential(r):
+            expw[r] = work.tile([P, WINDOW_ROWS, RUN], F32, name="expw")
+            nc.scalar.activation(out=expw[r][:], in_=window_view(cw_in[r]), func=ACT.Exp)
+
+        def product_and_rowsum(r):
+            prod[r] = work.tile([P, WINDOW_ROWS, RUN], F32, name="prod")
+            rowsum[r] = work.tile([P, 1], F32, name="rowsum")
             nc.vector.scalar_tensor_tensor(
-                out=prod[:],
-                in0=expw[:],
+                out=prod[r][:],
+                in0=expw[r][:],
                 scalar=1.0,
                 in1=window_view(mask_in[r]),
                 op0=ALU.mult,
                 op1=ALU.mult,
-                accum_out=rowsum[:],
+                accum_out=rowsum[r][:],
             )
-            rinv = work.tile([P, 1], F32, name="rinv")
-            nc.vector.reciprocal(out=rinv[:], in_=rowsum[:])
-            w_bf = work.tile([P, PACK, P], BF16, name="w_bf")
+
+        def reciprocal(r):
+            rinv[r] = work.tile([P, 1], F32, name="rinv")
+            nc.vector.reciprocal(out=rinv[r][:], in_=rowsum[r][:])
+
+        def normalise(r):
+            w_bf[r] = work.tile([P, PACK, P], BF16, name="w_bf")
             nc.vector.tensor_scalar(
-                out=w_bf[:].rearrange("g (u e) q -> g u e q", e=2),
-                in0=prod[:].rearrange("g a c -> g (a c)").rearrange("g (u q e) -> g u e q", u=2, e=2),
-                scalar1=rinv[:, 0:1],
+                out=w_bf[r][:].rearrange("g (u e) q -> g u e q", e=2),
+                in0=prod[r][:].rearrange("g a c -> g (a c)").rearrange("g (u q e) -> g u e q", u=2, e=2),
+                scalar1=rinv[r][:, 0:1],
                 scalar2=None,
                 op0=ALU.mult,
             )
-            wt = transposed.tile([P, PACK, P], BF16, name="wt", tag="bank")
+
+        def transpose_w(r):
+            wt[r] = transposed.tile([P, PACK, P], BF16, name="wt", tag="bank")
             for t in range(PACK):
-                nc.tensor.transpose(wt[:, t, :], w_bf[:, t, :], ident_bf[:])
-            w_grouped = work.tile([P, P, PACK], BF16, name="w_grouped", align_bytes=64)
-            nc.scalar.copy(out=w_grouped[:], in_=wt[:].rearrange("q t g -> q g t"))
+                nc.tensor.transpose(wt[r][:, t, :], w_bf[r][:, t, :], ident_bf[:])
+
+        def regroup_w(r):
+            w_grouped[r] = work.tile([P, P, PACK], BF16, name="w_grouped", align_bytes=64)
+            nc.scalar.copy(out=w_grouped[r][:], in_=wt[r][:].rearrange("q t g -> q g t"))
+
+        def quantise_w(r):
             nc.vector.quantize_mx(
                 out=w_codes[:, r * P : (r + 1) * P].bitcast(FP8X4),
                 scales=w_scales[:, r * P : (r + 1) * P],
-                in_=w_grouped[:].rearrange("q g t -> q (g t)"),
+                in_=w_grouped[r][:].rearrange("q g t -> q (g t)"),
             )
 
-        def prepare_x(n):
-            xc = work.tile([P, COLS], BF16, name="xc")
+        def gather_windows(n):
+            xc[n] = work.tile([P, COLS], BF16, name="xc")
             nc.vector.tensor_copy(
-                out=xc[:].rearrange("b (j r c) -> b j r c", j=2, c=RUN),
+                out=xc[n][:].rearrange("b (j r c) -> b j r c", j=2, c=RUN),
                 in_=x_in[n][:].rearrange("b (r j c) -> b j r c", j=2, c=RUN),
             )
-            xc_words = xc[:].bitcast(F32)
-            x_grouped = work.tile([P, COLS], BF16, name="x_grouped", align_bytes=64)
-            xg_words = x_grouped[:].bitcast(F32)
+
+        def transpose_x(n):
+            xc_words = xc[n][:].bitcast(F32)
             for j in range(2):
-                xt = transposed.tile([P, PACK, P], F32, name="xt", tag="bank")
+                xt[n, j] = transposed.tile([P, PACK, P], F32, name="xt", tag="bank")
                 for iu in range(PACK):
                     first = (j * PACK + iu) * P
-                    nc.tensor.transpose(xt[:, iu, :], xc_words[:, first : first + P], ident_f32[:])
+                    nc.tensor.transpose(xt[n, j][:, iu, :], xc_words[:, first : first + P], ident_f32[:])
+
+        def regroup_x(n):
+            x_grouped[n] = work.tile([P, COLS], BF16, name="x_grouped", align_bytes=64)
+            xg_words = x_grouped[n][:].bitcast(F32)
+            for j in range(2):
                 nc.scalar.copy(
                     out=xg_words[:, j * BANK : (j + 1) * BANK].rearrange("q (i b u) -> q i b u", i=2, u=2),
-                    in_=xt[:].rearrange("q (i u) b -> q i b u", u=2),
+                    in_=xt[n, j][:].rearrange("q (i u) b -> q i b u", u=2),
                 )
-            x_codes = work.tile([P, BANK], U32, name="x_codes", align_bytes=64)
-            x_scales = work.tile([P, BANK], U8, name="x_scales", align_bytes=64)
-            nc.vector.quantize_mx(out=x_codes[:].bitcast(FP8X4), scales=x_scales[:], in_=x_grouped[:])
-            return x_codes, x_scales
 
-        def multiply_and_store(n, x_codes, x_scales):
-            acc = [sums.tile([P, BANK], F32, name="acc%d" % b, tag="acc") for b in range(BANKS_OUT)]
+        def quantise_x(n):
+            x_codes[n] = work.tile([P, BANK], U32, name="x_codes", align_bytes=64)
+            x_scales[n] = work.tile([P, BANK], U8, name="x_scales", align_bytes=64)
+            nc.vector.quantize_mx(out=x_codes[n][:].bitcast(FP8X4), scales=x_scales[n][:], in_=x_grouped[n][:])
+
+        def multiply(n):
+            acc[n] = [sums.tile([P, BANK], F32, name="acc%d" % b, tag="acc") for b in range(BANKS_OUT)]
             for c0, c1 in zip(CUTS[:-1], CUTS[1:]):
                 i, j = divmod(c0 // G, 2)
                 slot = slice((2 * j + i) * P, (2 * j + i + 1) * P)
                 b = c0 // BANK
                 nc.tensor.matmul_mx(
-                    out=acc[b][:, c0 - b * BANK : c1 - b * BANK],
-                    lhsT=x_codes[:, slot].bitcast(FP8X4),
-                    lhsT_scale=x_scales[:, slot],
+                    out=acc[n][b][:, c0 - b * BANK : c1 - b * BANK],
+                    lhsT=x_codes[n][:, slot].bitcast(FP8X4),
+                    lhsT_scale=x_scales[n][:, slot],
                     rhs=w_codes[:, c0:c1].bitcast(FP8X4),
                     rhs_scale=w_scales[:, c0:c1],
                     start=True,
                     stop=True,
                 )
-            result = work.tile([P, OUT_COLS], F32, name="result")
-            for b in range(BANKS_OUT):
-                if (n * BANKS_OUT + b) % 2 == 0:
-                    nc.scalar.copy(out=result[:, b * BANK : (b + 1) * BANK], in_=acc[b][:])
-                else:
-                    nc.vector.tensor_copy(out=result[:, b * BANK : (b + 1) * BANK], in_=acc[b][:])
-            nc.sync.dma_start(out=out_rows[n * P : (n + 1) * P, :], in_=result[:])
 
-        ready = prepare_x(0)
-        for n in range(X_TILES):
-            following = prepare_x(n + 1) if n + 1 < X_TILES else None
-            multiply_and_store(n, ready[0], ready[1])
-            ready = following
+        def on_scalar(n, b):
+            return (n * BANKS_OUT + b) % 2 == 0
+
+        def empty_banks(n, scalar_turn):
+            if n not in result:
+                result[n] = results.tile([P, OUT_COLS], F32, name="result")
+            for b in range(BANKS_OUT):
+                if on_scalar(n, b) and scalar_turn:
+                    nc.scalar.copy(out=result[n][:, b * BANK : (b + 1) * BANK], in_=acc[n][b][:])
+                if not on_scalar(n, b) and not scalar_turn:
+                    nc.vector.tensor_copy(out=result[n][:, b * BANK : (b + 1) * BANK], in_=acc[n][b][:])
+
+        def store(n):
+            nc.sync.dma_start(out=out_rows[n * P : (n + 1) * P, :], in_=result[n][:])
+
+        def run(stage, index, count, *more):
+            if 0 <= index < count:
+                stage(index, *more)
+
+        for step in range(W_TILES + X_TILES + 3):
+            run(exponential, step, W_TILES)
+            run(product_and_rowsum, step - 1, W_TILES)
+            run(quantise_w, step - 4, W_TILES)
+            run(reciprocal, step - 1, W_TILES)
+            run(regroup_w, step - 3, W_TILES)
+            run(normalise, step - 2, W_TILES)
+            run(transpose_w, step - 2, W_TILES)
+
+            n = step - (W_TILES + 3)
+            run(multiply, n, X_TILES)
+            run(regroup_x, n + 1, X_TILES)
+            run(gather_windows, n + 2, X_TILES)
+            run(transpose_x, n + 2, X_TILES)
+            run(quantise_x, n + 1, X_TILES)
+            run(empty_banks, n, X_TILES, False)
+            run(empty_banks, n, X_TILES, True)
+            run(store, n, X_TILES)

@@ -196,7 +196,7 @@ def tile_connectlayer_kernel(tc, x, connect_w, connect_mask, out):
             if 0 <= index < count:
                 stage(index, *more)
 
-        for step in range(W_TILES + X_TILES + 3):
+        for step in range(W_TILES + X_TILES + 4):
             run(exponential, step, W_TILES)
             run(product_and_rowsum, step - 1, W_TILES)
             run(quantise_w, step - 4, W_TILES)
@@ -205,12 +205,12 @@ def tile_connectlayer_kernel(tc, x, connect_w, connect_mask, out):
             run(normalise, step - 2, W_TILES)
             run(transpose_w, step - 2, W_TILES)
 
-            n = step - (W_TILES + 3)
-            run(multiply, n, X_TILES)
-            run(regroup_x, n + 1, X_TILES)
-            run(gather_windows, n + 2, X_TILES)
-            run(transpose_x, n + 2, X_TILES)
+            n = step - (W_TILES + 4)
+            run(gather_windows, n + 3, X_TILES)
             run(quantise_x, n + 1, X_TILES)
+            run(multiply, n + 1, X_TILES)
+            run(transpose_x, n + 3, X_TILES)
             run(empty_banks, n, X_TILES, False)
             run(empty_banks, n, X_TILES, True)
             run(store, n, X_TILES)
+            run(regroup_x, n + 2, X_TILES)

@@ -177,26 +177,21 @@ def tile_connectlayer_kernel(tc, x, connect_w, connect_mask, out):
                     stop=True,
                 )
 
-        def on_scalar(n, b):
-            return (n * BANKS_OUT + b) % 2 == 0
-
-        def empty_banks(n, scalar_turn):
-            if n not in result:
-                result[n] = results.tile([P, OUT_COLS], F32, name="result")
+        def empty_and_store(n):
+            result[n] = results.tile([P, OUT_COLS], F32, name="result")
             for b in range(BANKS_OUT):
-                if on_scalar(n, b) and scalar_turn:
-                    nc.scalar.copy(out=result[n][:, b * BANK : (b + 1) * BANK], in_=acc[n][b][:])
-                if not on_scalar(n, b) and not scalar_turn:
-                    nc.vector.tensor_copy(out=result[n][:, b * BANK : (b + 1) * BANK], in_=acc[n][b][:])
-
-        def store(n):
-            nc.sync.dma_start(out=out_rows[n * P : (n + 1) * P, :], in_=result[n][:])
+                cols = slice(b * BANK, (b + 1) * BANK)
+                if (n * BANKS_OUT + b) % 2 == 0:
+                    nc.scalar.copy(out=result[n][:, cols], in_=acc[n][b][:])
+                else:
+                    nc.vector.tensor_copy(out=result[n][:, cols], in_=acc[n][b][:])
+                nc.sync.dma_start(out=out_rows[n * P : (n + 1) * P, cols], in_=result[n][:, cols])
 
         def run(stage, index, count, *more):
             if 0 <= index < count:
                 stage(index, *more)
 
-        for step in range(W_TILES + X_TILES + 4):
+        for step in range(W_TILES + X_TILES + 3):
             run(exponential, step, W_TILES)
             run(product_and_rowsum, step - 1, W_TILES)
             run(quantise_w, step - 4, W_TILES)
@@ -205,12 +200,10 @@ def tile_connectlayer_kernel(tc, x, connect_w, connect_mask, out):
             run(normalise, step - 2, W_TILES)
             run(transpose_w, step - 2, W_TILES)
 
-            n = step - (W_TILES + 4)
+            n = step - (W_TILES + 3)
+            run(multiply, n, X_TILES)
             run(gather_windows, n + 3, X_TILES)
-            run(quantise_x, n + 1, X_TILES)
-            run(multiply, n + 1, X_TILES)
             run(transpose_x, n + 3, X_TILES)
-            run(empty_banks, n, X_TILES, False)
-            run(empty_banks, n, X_TILES, True)
-            run(store, n, X_TILES)
             run(regroup_x, n + 2, X_TILES)
+            run(quantise_x, n + 1, X_TILES)
+            run(empty_and_store, n, X_TILES)

@@ -15,18 +15,19 @@ P = 128
 PACK = 4
 K = P * PACK
 BANK = 512
+PSUM_BANKS = 8
 
 BATCH = 1024
 COLS = 2048
 PIXEL_ROWS = 16
 ROW = COLS // PIXEL_ROWS
-RUN = ROW // 2
+SEGMENT = ROW // 2
 WINDOW_ROWS = PIXEL_ROWS // 2
 WINDOWS = 4
 G = 384
 OUT_COLS = WINDOWS * G
 HALF = COLS // 2
-SPAN = HALF - RUN
+SPAN = HALF - SEGMENT
 
 W_TILES = OUT_COLS // P
 X_TILES = BATCH // P
@@ -34,12 +35,17 @@ BANKS_OUT = OUT_COLS // BANK
 
 CUTS = sorted(set(range(0, OUT_COLS + 1, G)) | set(range(0, OUT_COLS + 1, BANK // 2)))
 
+TRANSPOSE_BANKS = 3
+SUM_BANKS = PSUM_BANKS - TRANSPOSE_BANKS
+WORK_BUFS = 3
+RESULT_BUFS = 4
+
 FLOPS = 2 * BATCH * OUT_COLS * K
 BYTES = 2 * BATCH * COLS + 2 * 2 * OUT_COLS * K + 4 * BATCH * OUT_COLS
 
 
 def window_view(half_rows):
-    return half_rows[:].rearrange("g (a s) -> g a s", s=ROW)[:, :, 0:RUN]
+    return half_rows[:].rearrange("g (a s) -> g a s", s=ROW)[:, :, 0:SEGMENT]
 
 
 def tile_connectlayer_kernel(tc, x, connect_w, connect_mask, out):
@@ -50,10 +56,10 @@ def tile_connectlayer_kernel(tc, x, connect_w, connect_mask, out):
         const = ctx.enter_context(tc.tile_pool(name="const", bufs=1))
         loads = ctx.enter_context(tc.tile_pool(name="loads", bufs=1))
         keep = ctx.enter_context(tc.tile_pool(name="keep", bufs=1))
-        work = ctx.enter_context(tc.tile_pool(name="work", bufs=3))
-        results = ctx.enter_context(tc.tile_pool(name="results", bufs=4))
-        transposed = ctx.enter_context(tc.psum_pool(name="transposed", bufs=3))
-        sums = ctx.enter_context(tc.psum_pool(name="sums", bufs=5))
+        work = ctx.enter_context(tc.tile_pool(name="work", bufs=WORK_BUFS))
+        results = ctx.enter_context(tc.tile_pool(name="results", bufs=RESULT_BUFS))
+        transposed = ctx.enter_context(tc.psum_pool(name="transposed", bufs=TRANSPOSE_BANKS))
+        sums = ctx.enter_context(tc.psum_pool(name="sums", bufs=SUM_BANKS))
         ctx.enter_context(tc.manual_schedule())
 
         cw_in = []
@@ -61,7 +67,7 @@ def tile_connectlayer_kernel(tc, x, connect_w, connect_mask, out):
         for r in range(W_TILES):
             i, j = divmod(r * P // G, 2)
             rows = slice(r * P, (r + 1) * P)
-            cols = slice(i * HALF + j * RUN, i * HALF + j * RUN + SPAN)
+            cols = slice(i * HALF + j * SEGMENT, i * HALF + j * SEGMENT + SPAN)
             cw_t = loads.tile([P, HALF], BF16, name="cw%d" % r)
             nc.sync.dma_start(out=cw_t[:, 0:SPAN], in_=connect_w[rows, cols])
             mask_t = loads.tile([P, HALF], BF16, name="mask%d" % r)
@@ -86,11 +92,11 @@ def tile_connectlayer_kernel(tc, x, connect_w, connect_mask, out):
         xc, xt, x_grouped, x_codes, x_scales, acc, result = {}, {}, {}, {}, {}, {}, {}
 
         def exponential(r):
-            expw[r] = work.tile([P, WINDOW_ROWS, RUN], F32, name="expw")
+            expw[r] = work.tile([P, WINDOW_ROWS, SEGMENT], F32, name="expw")
             nc.scalar.activation(out=expw[r][:], in_=window_view(cw_in[r]), func=ACT.Exp)
 
         def product_and_rowsum(r):
-            prod[r] = work.tile([P, WINDOW_ROWS, RUN], F32, name="prod")
+            prod[r] = work.tile([P, WINDOW_ROWS, SEGMENT], F32, name="prod")
             rowsum[r] = work.tile([P, 1], F32, name="rowsum")
             nc.vector.scalar_tensor_tensor(
                 out=prod[r][:],
@@ -135,24 +141,24 @@ def tile_connectlayer_kernel(tc, x, connect_w, connect_mask, out):
         def gather_windows(n):
             xc[n] = work.tile([P, COLS], BF16, name="xc")
             nc.vector.tensor_copy(
-                out=xc[n][:].rearrange("b (j r c) -> b j r c", j=2, c=RUN),
-                in_=x_in[n][:].rearrange("b (r j c) -> b j r c", j=2, c=RUN),
+                out=xc[n][:].rearrange("b (j r c) -> b j r c", j=2, c=SEGMENT),
+                in_=x_in[n][:].rearrange("b (r j c) -> b j r c", j=2, c=SEGMENT),
             )
 
         def transpose_x(n):
-            xc_words = xc[n][:].bitcast(F32)
+            pairs = xc[n][:].bitcast(F32)
             for j in range(2):
                 xt[n, j] = transposed.tile([P, PACK, P], F32, name="xt", tag="bank")
                 for iu in range(PACK):
                     first = (j * PACK + iu) * P
-                    nc.tensor.transpose(xt[n, j][:, iu, :], xc_words[:, first : first + P], ident_f32[:])
+                    nc.tensor.transpose(xt[n, j][:, iu, :], pairs[:, first : first + P], ident_f32[:])
 
         def regroup_x(n):
             x_grouped[n] = work.tile([P, COLS], BF16, name="x_grouped", align_bytes=64)
-            xg_words = x_grouped[n][:].bitcast(F32)
+            grouped_pairs = x_grouped[n][:].bitcast(F32)
             for j in range(2):
                 nc.scalar.copy(
-                    out=xg_words[:, j * BANK : (j + 1) * BANK].rearrange("q (i b u) -> q i b u", i=2, u=2),
+                    out=grouped_pairs[:, j * BANK : (j + 1) * BANK].rearrange("q (i b u) -> q i b u", i=2, u=2),
                     in_=xt[n, j][:].rearrange("q (i u) b -> q i b u", u=2),
                 )
 
@@ -165,12 +171,12 @@ def tile_connectlayer_kernel(tc, x, connect_w, connect_mask, out):
             acc[n] = [sums.tile([P, BANK], F32, name="acc%d" % b, tag="acc") for b in range(BANKS_OUT)]
             for c0, c1 in zip(CUTS[:-1], CUTS[1:]):
                 i, j = divmod(c0 // G, 2)
-                slot = slice((2 * j + i) * P, (2 * j + i + 1) * P)
+                window_cols = slice((2 * j + i) * P, (2 * j + i + 1) * P)
                 b = c0 // BANK
                 nc.tensor.matmul_mx(
                     out=acc[n][b][:, c0 - b * BANK : c1 - b * BANK],
-                    lhsT=x_codes[n][:, slot].bitcast(FP8X4),
-                    lhsT_scale=x_scales[n][:, slot],
+                    lhsT=x_codes[n][:, window_cols].bitcast(FP8X4),
+                    lhsT_scale=x_scales[n][:, window_cols],
                     rhs=w_codes[:, c0:c1].bitcast(FP8X4),
                     rhs_scale=w_scales[:, c0:c1],
                     start=True,
@@ -185,25 +191,26 @@ def tile_connectlayer_kernel(tc, x, connect_w, connect_mask, out):
                     nc.scalar.copy(out=result[n][:, cols], in_=acc[n][b][:])
                 else:
                     nc.vector.tensor_copy(out=result[n][:, cols], in_=acc[n][b][:])
-                nc.sync.dma_start(out=out_rows[n * P : (n + 1) * P, cols], in_=result[n][:, cols])
+            nc.sync.dma_start(out=out_rows[n * P : (n + 1) * P, :], in_=result[n][:])
 
-        def run(stage, index, count, *more):
+        def stage_if(stage, index, count):
             if 0 <= index < count:
-                stage(index, *more)
+                stage(index)
 
-        for step in range(W_TILES + X_TILES + 3):
-            run(exponential, step, W_TILES)
-            run(product_and_rowsum, step - 1, W_TILES)
-            run(quantise_w, step - 4, W_TILES)
-            run(reciprocal, step - 1, W_TILES)
-            run(regroup_w, step - 3, W_TILES)
-            run(normalise, step - 2, W_TILES)
-            run(transpose_w, step - 2, W_TILES)
+        first_passes = W_TILES + 3
+        for step in range(first_passes + X_TILES):
+            stage_if(exponential, step, W_TILES)
+            stage_if(product_and_rowsum, step - 1, W_TILES)
+            stage_if(quantise_w, step - 4, W_TILES)
+            stage_if(reciprocal, step - 1, W_TILES)
+            stage_if(regroup_w, step - 3, W_TILES)
+            stage_if(normalise, step - 2, W_TILES)
+            stage_if(transpose_w, step - 2, W_TILES)
 
-            n = step - (W_TILES + 3)
-            run(multiply, n, X_TILES)
-            run(gather_windows, n + 3, X_TILES)
-            run(transpose_x, n + 3, X_TILES)
-            run(regroup_x, n + 2, X_TILES)
-            run(quantise_x, n + 1, X_TILES)
-            run(empty_and_store, n, X_TILES)
+            n = step - first_passes
+            stage_if(multiply, n, X_TILES)
+            stage_if(gather_windows, n + 3, X_TILES)
+            stage_if(transpose_x, n + 3, X_TILES)
+            stage_if(regroup_x, n + 2, X_TILES)
+            stage_if(quantise_x, n + 1, X_TILES)
+            stage_if(empty_and_store, n, X_TILES)

@@ -191,7 +191,10 @@ def tile_connectlayer_kernel(tc, x, connect_w, connect_mask, out):
                     nc.scalar.copy(out=result[n][:, cols], in_=acc[n][b][:])
                 else:
                     nc.vector.tensor_copy(out=result[n][:, cols], in_=acc[n][b][:])
-            nc.sync.dma_start(out=out_rows[n * P : (n + 1) * P, :], in_=result[n][:])
+                if n == X_TILES - 1:
+                    nc.sync.dma_start(out=out_rows[n * P : (n + 1) * P, cols], in_=result[n][:, cols])
+            if n < X_TILES - 1:
+                nc.sync.dma_start(out=out_rows[n * P : (n + 1) * P, :], in_=result[n][:])
 
         def stage_if(stage, index, count):
             if 0 <= index < count:

from contextlib import ExitStack

import concourse.mybir as mybir
from concourse.masks import make_identity

F32 = mybir.dt.float32
BF16 = mybir.dt.bfloat16
U32 = mybir.dt.uint32
U8 = mybir.dt.uint8
FP8X4 = mybir.dt.float8_e4m3fn_x4
ACT = mybir.ActivationFunctionType
ALU = mybir.AluOpType

P = 128
PACK = 4
K = P * PACK
BANK = 512
PSUM_BANKS = 8

BATCH = 1024
COLS = 2048
PIXEL_ROWS = 16
ROW = COLS // PIXEL_ROWS
SEGMENT = ROW // 2
WINDOW_ROWS = PIXEL_ROWS // 2
WINDOWS = 4
G = 384
OUT_COLS = WINDOWS * G
HALF = COLS // 2
SPAN = HALF - SEGMENT

W_TILES = OUT_COLS // P
X_TILES = BATCH // P
BANKS_OUT = OUT_COLS // BANK

CUTS = sorted(set(range(0, OUT_COLS + 1, G)) | set(range(0, OUT_COLS + 1, BANK // 2)))

TRANSPOSE_BANKS = 3
SUM_BANKS = PSUM_BANKS - TRANSPOSE_BANKS
WORK_BUFS = 3
RESULT_BUFS = 4

FLOPS = 2 * BATCH * OUT_COLS * K
BYTES = 2 * BATCH * COLS + 2 * 2 * OUT_COLS * K + 4 * BATCH * OUT_COLS


def window_view(half_rows):
    return half_rows[:].rearrange("g (a s) -> g a s", s=ROW)[:, :, 0:SEGMENT]


def tile_connectlayer_kernel(tc, x, connect_w, connect_mask, out):
    nc = tc.nc
    out_rows = out.rearrange("b r s -> b (r s)")

    with ExitStack() as ctx:
        const = ctx.enter_context(tc.tile_pool(name="const", bufs=1))
        loads = ctx.enter_context(tc.tile_pool(name="loads", bufs=1))
        keep = ctx.enter_context(tc.tile_pool(name="keep", bufs=1))
        work = ctx.enter_context(tc.tile_pool(name="work", bufs=WORK_BUFS))
        results = ctx.enter_context(tc.tile_pool(name="results", bufs=RESULT_BUFS))
        transposed = ctx.enter_context(tc.psum_pool(name="transposed", bufs=TRANSPOSE_BANKS))
        sums = ctx.enter_context(tc.psum_pool(name="sums", bufs=SUM_BANKS))
        ctx.enter_context(tc.manual_schedule())

        cw_in = []
        mask_in = []
        for r in range(W_TILES):
            i, j = divmod(r * P // G, 2)
            rows = slice(r * P, (r + 1) * P)
            cols = slice(i * HALF + j * SEGMENT, i * HALF + j * SEGMENT + SPAN)
            cw_t = loads.tile([P, HALF], BF16, name="cw%d" % r)
            nc.sync.dma_start(out=cw_t[:, 0:SPAN], in_=connect_w[rows, cols])
            mask_t = loads.tile([P, HALF], BF16, name="mask%d" % r)
            nc.sync.dma_start(out=mask_t[:, 0:SPAN], in_=connect_mask[rows, cols])
            cw_in.append(cw_t)
            mask_in.append(mask_t)
        x_in = []
        for n in range(X_TILES):
            x_t = loads.tile([P, COLS], BF16, name="x%d" % n)
            nc.sync.dma_start(out=x_t[:], in_=x[n * P : (n + 1) * P, :])
            x_in.append(x_t)

        ident_bf = const.tile([P, P], BF16, name="ident_bf")
        make_identity(nc, ident_bf[:])
        ident_f32 = const.tile([P, P], F32, name="ident_f32")
        make_identity(nc, ident_f32[:])

        w_codes = keep.tile([P, OUT_COLS], U32, name="w_codes", align_bytes=64)
        w_scales = keep.tile([P, OUT_COLS], U8, name="w_scales", align_bytes=64)

        expw, prod, rowsum, rinv, w_bf, wt, w_grouped = {}, {}, {}, {}, {}, {}, {}
        xc, xt, x_grouped, x_codes, x_scales, acc, result = {}, {}, {}, {}, {}, {}, {}

        def exponential(r):
            expw[r] = work.tile([P, WINDOW_ROWS, SEGMENT], F32, name="expw")
            nc.scalar.activation(out=expw[r][:], in_=window_view(cw_in[r]), func=ACT.Exp)

        def product_and_rowsum(r):
            prod[r] = work.tile([P, WINDOW_ROWS, SEGMENT], F32, name="prod")
            rowsum[r] = work.tile([P, 1], F32, name="rowsum")
            nc.vector.scalar_tensor_tensor(
                out=prod[r][:],
                in0=expw[r][:],
                scalar=1.0,
                in1=window_view(mask_in[r]),
                op0=ALU.mult,
                op1=ALU.mult,
                accum_out=rowsum[r][:],
            )

        def reciprocal(r):
            rinv[r] = work.tile([P, 1], F32, name="rinv")
            nc.vector.reciprocal(out=rinv[r][:], in_=rowsum[r][:])

        def normalise(r):
            w_bf[r] = work.tile([P, PACK, P], BF16, name="w_bf")
            nc.vector.tensor_scalar(
                out=w_bf[r][:].rearrange("g (u e) q -> g u e q", e=2),
                in0=prod[r][:].rearrange("g a c -> g (a c)").rearrange("g (u q e) -> g u e q", u=2, e=2),
                scalar1=rinv[r][:, 0:1],
                scalar2=None,
                op0=ALU.mult,
            )

        def transpose_w(r):
            wt[r] = transposed.tile([P, PACK, P], BF16, name="wt", tag="bank")
            for t in range(PACK):
                nc.tensor.transpose(wt[r][:, t, :], w_bf[r][:, t, :], ident_bf[:])

        def regroup_w(r):
            w_grouped[r] = work.tile([P, P, PACK], BF16, name="w_grouped", align_bytes=64)
            nc.scalar.copy(out=w_grouped[r][:], in_=wt[r][:].rearrange("q t g -> q g t"))

        def quantise_w(r):
            nc.vector.quantize_mx(
                out=w_codes[:, r * P : (r + 1) * P].bitcast(FP8X4),
                scales=w_scales[:, r * P : (r + 1) * P],
                in_=w_grouped[r][:].rearrange("q g t -> q (g t)"),
            )

        def gather_windows(n):
            xc[n] = work.tile([P, COLS], BF16, name="xc")
            nc.vector.tensor_copy(
                out=xc[n][:].rearrange("b (j r c) -> b j r c", j=2, c=SEGMENT),
                in_=x_in[n][:].rearrange("b (r j c) -> b j r c", j=2, c=SEGMENT),
            )

        def transpose_x(n):
            pairs = xc[n][:].bitcast(F32)
            for j in range(2):
                xt[n, j] = transposed.tile([P, PACK, P], F32, name="xt", tag="bank")
                for iu in range(PACK):
                    first = (j * PACK + iu) * P
                    nc.tensor.transpose(xt[n, j][:, iu, :], pairs[:, first : first + P], ident_f32[:])

        def regroup_x(n):
            x_grouped[n] = work.tile([P, COLS], BF16, name="x_grouped", align_bytes=64)
            grouped_pairs = x_grouped[n][:].bitcast(F32)
            for j in range(2):
                nc.scalar.copy(
                    out=grouped_pairs[:, j * BANK : (j + 1) * BANK].rearrange("q (i b u) -> q i b u", i=2, u=2),
                    in_=xt[n, j][:].rearrange("q (i u) b -> q i b u", u=2),
                )

        def quantise_x(n):
            x_codes[n] = work.tile([P, BANK], U32, name="x_codes", align_bytes=64)
            x_scales[n] = work.tile([P, BANK], U8, name="x_scales", align_bytes=64)
            nc.vector.quantize_mx(out=x_codes[n][:].bitcast(FP8X4), scales=x_scales[n][:], in_=x_grouped[n][:])

        def multiply(n):
            acc[n] = [sums.tile([P, BANK], F32, name="acc%d" % b, tag="acc") for b in range(BANKS_OUT)]
            for c0, c1 in zip(CUTS[:-1], CUTS[1:]):
                i, j = divmod(c0 // G, 2)
                window_cols = slice((2 * j + i) * P, (2 * j + i + 1) * P)
                b = c0 // BANK
                nc.tensor.matmul_mx(
                    out=acc[n][b][:, c0 - b * BANK : c1 - b * BANK],
                    lhsT=x_codes[n][:, window_cols].bitcast(FP8X4),
                    lhsT_scale=x_scales[n][:, window_cols],
                    rhs=w_codes[:, c0:c1].bitcast(FP8X4),
                    rhs_scale=w_scales[:, c0:c1],
                    start=True,
                    stop=True,
                )

        def empty_and_store(n):
            result[n] = results.tile([P, OUT_COLS], F32, name="result")
            for b in range(BANKS_OUT):
                cols = slice(b * BANK, (b + 1) * BANK)
                if (n * BANKS_OUT + b) % 2 == 0:
                    nc.scalar.copy(out=result[n][:, cols], in_=acc[n][b][:])
                else:
                    nc.vector.tensor_copy(out=result[n][:, cols], in_=acc[n][b][:])
                if n == X_TILES - 1:
                    nc.sync.dma_start(out=out_rows[n * P : (n + 1) * P, cols], in_=result[n][:, cols])
            if n < X_TILES - 1:
                nc.sync.dma_start(out=out_rows[n * P : (n + 1) * P, :], in_=result[n][:])

        def stage_if(stage, index, count):
            if 0 <= index < count:
                stage(index)

        first_passes = W_TILES + 3
        for step in range(first_passes + X_TILES):
            stage_if(exponential, step, W_TILES)
            stage_if(product_and_rowsum, step - 1, W_TILES)
            stage_if(quantise_w, step - 4, W_TILES)
            stage_if(reciprocal, step - 1, W_TILES)
            stage_if(regroup_w, step - 3, W_TILES)
            stage_if(normalise, step - 2, W_TILES)
            stage_if(transpose_w, step - 2, W_TILES)

            n = step - first_passes
            stage_if(multiply, n, X_TILES)
            stage_if(gather_windows, n + 3, X_TILES)
            stage_if(transpose_x, n + 3, X_TILES)
            stage_if(regroup_x, n + 2, X_TILES)
            stage_if(quantise_x, n + 1, X_TILES)
            stage_if(empty_and_store, n, X_TILES)
